import numpy as np
import ml_dtypes


def mxq(x, axis, fmt="e4m3"):
    dtype, down = {"e4m3": (ml_dtypes.float8_e4m3fn, 7), "e5m2": (ml_dtypes.float8_e5m2, 14)}[fmt]
    v = np.moveaxis(np.asarray(x, np.float32).astype(ml_dtypes.bfloat16).astype(np.float64), axis, -1)
    blocks = v.reshape(v.shape[:-1] + (-1, 32))
    amax = np.abs(blocks).max(-1, keepdims=True)
    byte = np.maximum(np.where(amax > 0, np.frexp(amax)[1] - 1 + 127, 0) - down, 1)
    scale = np.exp2(byte - 127.0)
    codes = (blocks / scale).astype(np.float32).astype(dtype).astype(np.float64)
    return np.moveaxis((codes * scale).reshape(v.shape), -1, axis)


WIDE = False


def mx_kscale(k):
    if not WIDE:
        return np.ones(k)
    levels = np.array([10, -10, 5, -5, 0])
    a = np.random.permutation(np.resize(levels, k // 512 * 4)).reshape(k // 512, 4)
    idx = np.arange(k)
    return np.exp2(a[idx // 512, idx % 128 // 32])


BF16 = ml_dtypes.bfloat16


def bf(x):
    return np.asarray(x, np.float32).astype(BF16)


def f64(x):
    return np.asarray(x).astype(np.float64)


B, T, C, F = 1, 512, 256, 512
M = T
K = C + C


def silu(v):
    return v / (1.0 + np.exp(-v))


def setup_inputs():
    s = mx_kscale(K)
    u = s[:C]
    x = np.random.standard_normal((B, T, C)) + 0.5 * np.random.standard_normal((B, 1, C))
    return {"x": bf(x * u),
            "memory": bf(np.random.standard_normal((1, M, C)) * 6.0 / np.sqrt(C) / u),
            "w1": bf(np.random.standard_normal((K, F)) / np.sqrt(K) * np.concatenate([1.0 / u, u])[:, None]),
            "b1": bf(np.random.standard_normal(F) * 0.3)}


def reference(x, memory, w1, b1):
    energy = f64(x) @ f64(memory)[0].T
    e = np.exp(energy - energy.max(-1, keepdims=True))
    retrieved = (mxq(e, 2, "e4m3") @ mxq(f64(memory)[0], 0, "e4m3")) / e.sum(-1, keepdims=True)
    cat = np.concatenate([f64(x), retrieved], axis=-1)
    return silu((mxq(cat, 2, "e4m3") @ mxq(f64(w1), 0, "e4m3")) + f64(b1))

@@ -1,0 +1,175 @@
+from contextlib import ExitStack
+
+import concourse.mybir as mybir
+from concourse.masks import make_identity
+
+BF16 = mybir.dt.bfloat16
+F32 = mybir.dt.float32
+U32 = mybir.dt.uint32
+U8 = mybir.dt.uint8
+FP8X4 = mybir.dt.float8_e4m3fn_x4
+ACT = mybir.ActivationFunctionType
+ALU = mybir.AluOpType
+AXIS = mybir.AxisListType
+
+P = 128
+PACK = 4
+T, C, M, F = 512, 256, 512, 512
+TILES = T // P
+HALVES = C // P
+HALF_P = P // 2
+VECTOR_TILES = 2
+
+FLOPS = 2 * T * M * C + 2 * T * M * C + 2 * T * (2 * C) * F
+
+
+def tile_dynamicmemorybank_pa_s_kernel(tc, x, memory, w1, b1, out):
+    nc = tc.nc
+    with ExitStack() as ctx:
+        keep = ctx.enter_context(tc.tile_pool(name="keep", bufs=1))
+        turned = ctx.enter_context(tc.psum_pool(name="turned", bufs=4))
+        sums = ctx.enter_context(tc.psum_pool(name="sums", bufs=4))
+
+        mem_sb = keep.tile([P, PACK, C], BF16)
+        nc.sync.dma_start(out=mem_sb[:], in_=memory[0].rearrange("(p j) c -> p j c", j=PACK))
+        x_sb = keep.tile([P, TILES, C], BF16)
+        nc.sync.dma_start(out=x_sb[:], in_=x[0].rearrange("(p i) c -> p i c", i=TILES))
+        w1_sb = keep.tile([P, PACK, F], BF16)
+        nc.sync.dma_start(out=w1_sb[:], in_=w1.rearrange("(p j) f -> p j f", j=PACK))
+        b1_all = keep.tile([P, F], BF16)
+        nc.sync.dma_start(out=b1_all[:], in_=b1.partition_broadcast(P))
+
+        ident = keep.tile([P, P], BF16)
+        make_identity(nc, ident[:])
+
+        warm_in = keep.tile([P, 1], F32)
+        warm_out = keep.tile([P, 1], F32)
+        nc.vector.memset(warm_in[:], 0.0)
+        nc.scalar.activation(out=warm_out[:], in_=warm_in[:], func=ACT.Exp)
+
+        def transpose_four(blocks):
+            flipped = turned.tile([P, PACK, P], BF16, name="flipped", tag="flipped")
+            for j in range(PACK):
+                nc.tensor.transpose(flipped[:, j, :], blocks[j], ident[:])
+            return flipped
+
+        def copy_out(i, dst, src):
+            if i < VECTOR_TILES:
+                nc.vector.tensor_copy(out=dst, in_=src)
+            else:
+                nc.scalar.copy(out=dst, in_=src)
+
+        memT = keep.tile([P, HALVES, M], BF16)
+        xT = keep.tile([P, HALVES, T], BF16)
+        for src, dst in ((mem_sb, memT), (x_sb, xT)):
+            for h in range(HALVES):
+                flipped = transpose_four([src[:, j, h * P : (h + 1) * P] for j in range(PACK)])
+                nc.scalar.copy(out=dst[:, h, :], in_=flipped[:].rearrange("p j q -> p (j q)"))
+
+        mem_grp = keep.tile([P, C, PACK], BF16, align_bytes=64)
+        mem_q = keep.tile([P, C], U32, align_bytes=64)
+        mem_s = keep.tile([P, C], U8, align_bytes=64)
+        nc.vector.tensor_copy(out=mem_grp[:], in_=mem_sb[:].rearrange("p j c -> p c j"))
+
+        cat = keep.tile([P, TILES, PACK, P], BF16)
+        nc.vector.tensor_copy(
+            out=cat[:, :, :, 0:HALF_P], in_=x_sb[:].rearrange("p i (q j) -> p i j q", j=PACK)
+        )
+        nc.vector.quantize_mx(
+            out=mem_q[:].bitcast(FP8X4), scales=mem_s[:], in_=mem_grp[:].rearrange("p c j -> p (c j)")
+        )
+
+        w1_grp = keep.tile([P, F, PACK], BF16, align_bytes=64)
+        w1_q = keep.tile([P, F], U32, align_bytes=64)
+        w1_s = keep.tile([P, F], U8, align_bytes=64)
+        nc.vector.tensor_copy(out=w1_grp[:], in_=w1_sb[:].rearrange("p j f -> p f j"))
+        nc.vector.quantize_mx(
+            out=w1_q[:].bitcast(FP8X4), scales=w1_s[:], in_=w1_grp[:].rearrange("p f j -> p (f j)")
+        )
+
+        neg_max = keep.tile([P, TILES], F32)
+        row_sum = keep.tile([P, TILES], F32)
+        inv_sum = keep.tile([P, TILES], F32)
+        e_sb = keep.tile([P, TILES, M], BF16)
+        for i in range(TILES):
+            energy = sums.tile([P, M], F32, name="energy", tag="sums")
+            for h in range(HALVES):
+                nc.tensor.matmul(
+                    energy[:],
+                    lhsT=xT[:, h, i * P : (i + 1) * P],
+                    rhs=memT[:, h, :],
+                    start=(h == 0),
+                    stop=(h == HALVES - 1),
+                )
+            nc.vector.tensor_reduce(
+                out=neg_max[:, i : i + 1], in_=energy[:], axis=AXIS.X, op=ALU.max, negate=True
+            )
+            nc.scalar.activation(
+                out=e_sb[:, i, :],
+                in_=energy[:],
+                func=ACT.Exp,
+                bias=neg_max[:, i : i + 1],
+                scale=1.0,
+                accum_out=row_sum[:, i : i + 1],
+            )
+            nc.vector.reciprocal(inv_sum[:, i : i + 1], row_sum[:, i : i + 1])
+
+        e_grp = keep.tile([P, TILES, P, PACK], BF16, align_bytes=64)
+        e_q = keep.tile([P, TILES, P], U32, align_bytes=64)
+        e_s = keep.tile([P, TILES, P], U8, align_bytes=64)
+        for i in range(TILES):
+            flipped = transpose_four([e_sb[:, i, j * P : (j + 1) * P] for j in range(PACK)])
+            copy_out(i, e_grp[:, i], flipped[:].rearrange("p j t -> p t j"))
+            nc.vector.quantize_mx(
+                out=e_q[:, i, :].bitcast(FP8X4),
+                scales=e_s[:, i, :],
+                in_=e_grp[:, i].rearrange("p t j -> p (t j)"),
+            )
+
+        for i in range(TILES):
+            read = sums.tile([P, C], F32, name="read", tag="sums")
+            nc.tensor.matmul_mx(
+                out=read[:],
+                lhsT=e_q[:, i, :].bitcast(FP8X4),
+                lhsT_scale=e_s[:, i, :],
+                rhs=mem_q[:].bitcast(FP8X4),
+                rhs_scale=mem_s[:],
+                start=True,
+                stop=True,
+            )
+            nc.scalar.activation(
+                out=cat[:, i, :, HALF_P:P],
+                in_=read[:].rearrange("p (q j) -> p j q", j=PACK),
+                func=ACT.Copy,
+                scale=inv_sum[:, i : i + 1],
+            )
+
+        cat_grp = keep.tile([P, TILES, P, PACK], BF16, align_bytes=64)
+        cat_q = keep.tile([P, TILES, P], U32, align_bytes=64)
+        cat_s = keep.tile([P, TILES, P], U8, align_bytes=64)
+        for i in range(TILES):
+            flipped = transpose_four([cat[:, i, j, :] for j in range(PACK)])
+            copy_out(i, cat_grp[:, i], flipped[:].rearrange("p j t -> p t j"))
+            nc.vector.quantize_mx(
+                out=cat_q[:, i, :].bitcast(FP8X4),
+                scales=cat_s[:, i, :],
+                in_=cat_grp[:, i].rearrange("p t j -> p (t j)"),
+            )
+
+        out_rows = out[0].rearrange("(p i) f -> p i f", i=TILES)
+        biased = keep.tile([P, TILES, F], F32)
+        result = keep.tile([P, TILES, F], F32)
+        for i in range(TILES):
+            fused = sums.tile([P, F], F32, name="fused", tag="sums")
+            nc.tensor.matmul_mx(
+                out=fused[:],
+                lhsT=cat_q[:, i, :].bitcast(FP8X4),
+                lhsT_scale=cat_s[:, i, :],
+                rhs=w1_q[:].bitcast(FP8X4),
+                rhs_scale=w1_s[:],
+                start=True,
+                stop=True,
+            )
+            nc.vector.tensor_tensor(out=biased[:, i, :], in0=fused[:], in1=b1_all[:], op=ALU.add)
+            nc.scalar.activation(out=result[:, i, :], in_=biased[:, i, :], func=ACT.Silu)
+            nc.sync.dma_start(out=out_rows[:, i, :], in_=result[:, i, :])

@@ -16,8 +16,7 @@ P = 128
 PACK = 4
 T, C, M, F = 512, 256, 512, 512
 TILES = T // P
-HALVES = C // P
-HALF_P = P // 2
+PAIR = 2
 VECTOR_TILES = 2
 
 FLOPS = 2 * T * M * C + 2 * T * M * C + 2 * T * (2 * C) * F
@@ -32,14 +31,14 @@ def tile_dynamicmemorybank_pa_s_kernel(tc, x, memory, w1, b1, out):
 
         mem_sb = keep.tile([P, PACK, C], BF16)
         nc.sync.dma_start(out=mem_sb[:], in_=memory[0].rearrange("(p j) c -> p j c", j=PACK))
-        x_sb = keep.tile([P, TILES, C], BF16)
-        nc.sync.dma_start(out=x_sb[:], in_=x[0].rearrange("(p i) c -> p i c", i=TILES))
+        cat = keep.tile([P, TILES, 2 * C], BF16)
+        nc.sync.dma_start(out=cat[:, :, 0:C], in_=x[0].rearrange("(p i) c -> p i c", i=TILES))
         w1_sb = keep.tile([P, PACK, F], BF16)
         nc.sync.dma_start(out=w1_sb[:], in_=w1.rearrange("(p j) f -> p j f", j=PACK))
         b1_all = keep.tile([P, F], BF16)
         nc.sync.dma_start(out=b1_all[:], in_=b1.partition_broadcast(P))
 
-        ident = keep.tile([P, P], BF16)
+        ident = keep.tile([P, P], F32)
         make_identity(nc, ident[:])
 
         warm_in = keep.tile([P, 1], F32)
@@ -47,10 +46,10 @@ def tile_dynamicmemorybank_pa_s_kernel(tc, x, memory, w1, b1, out):
         nc.vector.memset(warm_in[:], 0.0)
         nc.scalar.activation(out=warm_out[:], in_=warm_in[:], func=ACT.Exp)
 
-        def transpose_four(blocks):
-            flipped = turned.tile([P, PACK, P], BF16, name="flipped", tag="flipped")
-            for j in range(PACK):
-                nc.tensor.transpose(flipped[:, j, :], blocks[j], ident[:])
+        def transpose_pair(blocks):
+            flipped = turned.tile([P, PAIR, P], F32, name="flipped", tag="flipped")
+            for u in range(PAIR):
+                nc.tensor.transpose(flipped[:, u, :], blocks[u], ident[:])
             return flipped
 
         def copy_out(i, dst, src):
@@ -59,22 +58,26 @@ def tile_dynamicmemorybank_pa_s_kernel(tc, x, memory, w1, b1, out):
             else:
                 nc.scalar.copy(out=dst, in_=src)
 
-        memT = keep.tile([P, HALVES, M], BF16)
-        xT = keep.tile([P, HALVES, T], BF16)
-        for src, dst in ((mem_sb, memT), (x_sb, xT)):
-            for h in range(HALVES):
-                flipped = transpose_four([src[:, j, h * P : (h + 1) * P] for j in range(PACK)])
-                nc.scalar.copy(out=dst[:, h, :], in_=flipped[:].rearrange("p j q -> p (j q)"))
+        memT = keep.tile([P, M], F32)
+        for u in range(PAIR):
+            flipped = transpose_pair([mem_sb[:, PAIR * u + v, :].bitcast(F32) for v in range(PAIR)])
+            nc.scalar.copy(
+                out=memT[:, u * PAIR * P : (u + 1) * PAIR * P].rearrange("w (p v) -> w p v", v=PAIR),
+                in_=flipped[:].rearrange("w v p -> w p v"),
+            )
+        xT = keep.tile([P, T], F32)
+        for g in range(TILES // PAIR):
+            flipped = transpose_pair([cat[:, PAIR * g + r, 0:C].bitcast(F32) for r in range(PAIR)])
+            nc.scalar.copy(
+                out=xT[:, g * PAIR * P : (g + 1) * PAIR * P], in_=flipped[:].rearrange("w r p -> w (r p)")
+            )
+        memT_half = memT[:].bitcast(BF16).rearrange("w (m h) -> w h m", h=PAIR)
+        xT_half = xT[:].bitcast(BF16).rearrange("w (t h) -> w h t", h=PAIR)
 
         mem_grp = keep.tile([P, C, PACK], BF16, align_bytes=64)
         mem_q = keep.tile([P, C], U32, align_bytes=64)
         mem_s = keep.tile([P, C], U8, align_bytes=64)
         nc.vector.tensor_copy(out=mem_grp[:], in_=mem_sb[:].rearrange("p j c -> p c j"))
-
-        cat = keep.tile([P, TILES, PACK, P], BF16)
-        nc.vector.tensor_copy(
-            out=cat[:, :, :, 0:HALF_P], in_=x_sb[:].rearrange("p i (q j) -> p i j q", j=PACK)
-        )
         nc.vector.quantize_mx(
             out=mem_q[:].bitcast(FP8X4), scales=mem_s[:], in_=mem_grp[:].rearrange("p c j -> p (c j)")
         )
@@ -93,13 +96,13 @@ def tile_dynamicmemorybank_pa_s_kernel(tc, x, memory, w1, b1, out):
         e_sb = keep.tile([P, TILES, M], BF16)
         for i in range(TILES):
             energy = sums.tile([P, M], F32, name="energy", tag="sums")
-            for h in range(HALVES):
+            for h in range(PAIR):
                 nc.tensor.matmul(
                     energy[:],
-                    lhsT=xT[:, h, i * P : (i + 1) * P],
-                    rhs=memT[:, h, :],
+                    lhsT=xT_half[:, h, i * P : (i + 1) * P],
+                    rhs=memT_half[:, h, :],
                     start=(h == 0),
-                    stop=(h == HALVES - 1),
+                    stop=(h == PAIR - 1),
                 )
             nc.vector.tensor_reduce(
                 out=neg_max[:, i : i + 1], in_=energy[:], axis=AXIS.X, op=ALU.max, negate=True
@@ -114,16 +117,17 @@ def tile_dynamicmemorybank_pa_s_kernel(tc, x, memory, w1, b1, out):
             )
             nc.vector.reciprocal(inv_sum[:, i : i + 1], row_sum[:, i : i + 1])
 
-        e_grp = keep.tile([P, TILES, P, PACK], BF16, align_bytes=64)
+        e_grp = keep.tile([P, TILES, P, PAIR], F32, align_bytes=64)
         e_q = keep.tile([P, TILES, P], U32, align_bytes=64)
         e_s = keep.tile([P, TILES, P], U8, align_bytes=64)
         for i in range(TILES):
-            flipped = transpose_four([e_sb[:, i, j * P : (j + 1) * P] for j in range(PACK)])
-            copy_out(i, e_grp[:, i], flipped[:].rearrange("p j t -> p t j"))
+            e_words = e_sb[:, i, :].bitcast(F32)
+            flipped = transpose_pair([e_words[:, u * P : (u + 1) * P] for u in range(PAIR)])
+            copy_out(i, e_grp[:, i], flipped[:].rearrange("p u t -> p t u"))
             nc.vector.quantize_mx(
                 out=e_q[:, i, :].bitcast(FP8X4),
                 scales=e_s[:, i, :],
-                in_=e_grp[:, i].rearrange("p t j -> p (t j)"),
+                in_=e_grp[:, i].rearrange("p t u -> p (t u)").bitcast(BF16),
             )
 
         for i in range(TILES):
@@ -138,22 +142,23 @@ def tile_dynamicmemorybank_pa_s_kernel(tc, x, memory, w1, b1, out):
                 stop=True,
             )
             nc.scalar.activation(
-                out=cat[:, i, :, HALF_P:P],
-                in_=read[:].rearrange("p (q j) -> p j q", j=PACK),
+                out=cat[:, i, C : 2 * C],
+                in_=read[:],
                 func=ACT.Copy,
                 scale=inv_sum[:, i : i + 1],
             )
 
-        cat_grp = keep.tile([P, TILES, P, PACK], BF16, align_bytes=64)
+        cat_grp = keep.tile([P, TILES, P, PAIR], F32, align_bytes=64)
         cat_q = keep.tile([P, TILES, P], U32, align_bytes=64)
         cat_s = keep.tile([P, TILES, P], U8, align_bytes=64)
         for i in range(TILES):
-            flipped = transpose_four([cat[:, i, j, :] for j in range(PACK)])
-            copy_out(i, cat_grp[:, i], flipped[:].rearrange("p j t -> p t j"))
+            cat_words = cat[:, i, :].bitcast(F32).rearrange("p (q u) -> p u q", u=PAIR)
+            flipped = transpose_pair([cat_words[:, u, :] for u in range(PAIR)])
+            copy_out(i, cat_grp[:, i], flipped[:].rearrange("q u t -> q t u"))
             nc.vector.quantize_mx(
                 out=cat_q[:, i, :].bitcast(FP8X4),
                 scales=cat_s[:, i, :],
-                in_=cat_grp[:, i].rearrange("p t j -> p (t j)"),
+                in_=cat_grp[:, i].rearrange("q t u -> q (t u)").bitcast(BF16),
             )
 
         out_rows = out[0].rearrange("(p i) f -> p i f", i=TILES)

@@ -30,9 +30,13 @@ def tile_dynamicmemorybank_pa_s_kernel(tc, x, memory, w1, b1, out):
         sums = ctx.enter_context(tc.psum_pool(name="sums", bufs=4))
 
         mem_sb = keep.tile([P, PACK, C], BF16)
-        nc.sync.dma_start(out=mem_sb[:], in_=memory[0].rearrange("(p j) c -> p j c", j=PACK))
+        mem_rows = memory[0].rearrange("(p j) c -> p j c", j=PACK)
         cat = keep.tile([P, TILES, 2 * C], BF16)
-        nc.sync.dma_start(out=cat[:, :, 0:C], in_=x[0].rearrange("(p i) c -> p i c", i=TILES))
+        x_rows = x[0].rearrange("(p i) c -> p i c", i=TILES)
+        nc.sync.dma_start(out=mem_sb[:, 0:PAIR, :], in_=mem_rows[:, 0:PAIR, :])
+        nc.sync.dma_start(out=mem_sb[:, PAIR:PACK, :], in_=mem_rows[:, PAIR:PACK, :])
+        nc.sync.dma_start(out=cat[:, 0:PAIR, 0:C], in_=x_rows[:, 0:PAIR, :])
+        nc.sync.dma_start(out=cat[:, PAIR:TILES, 0:C], in_=x_rows[:, PAIR:TILES, :])
         w1_sb = keep.tile([P, PACK, F], BF16)
         nc.sync.dma_start(out=w1_sb[:], in_=w1.rearrange("(p j) f -> p j f", j=PACK))
         b1_all = keep.tile([P, F], BF16)
@@ -42,9 +46,9 @@ def tile_dynamicmemorybank_pa_s_kernel(tc, x, memory, w1, b1, out):
         make_identity(nc, ident[:])
 
         warm_in = keep.tile([P, 1], F32)
-        warm_out = keep.tile([P, 1], F32)
+        warm_out = keep.tile([P, PAIR], F32)
         nc.vector.memset(warm_in[:], 0.0)
-        nc.scalar.activation(out=warm_out[:], in_=warm_in[:], func=ACT.Exp)
+        nc.scalar.activation(out=warm_out[:, 0:1], in_=warm_in[:], func=ACT.Exp)
 
         def transpose_pair(blocks):
             flipped = turned.tile([P, PAIR, P], F32, name="flipped", tag="flipped")
@@ -147,6 +151,7 @@ def tile_dynamicmemorybank_pa_s_kernel(tc, x, memory, w1, b1, out):
                 func=ACT.Copy,
                 scale=inv_sum[:, i : i + 1],
             )
+        nc.scalar.activation(out=warm_out[:, 1:2], in_=cat[:, TILES - 1, 2 * C - 1 : 2 * C], func=ACT.Silu)
 
         cat_grp = keep.tile([P, TILES, P, PAIR], F32, align_bytes=64)
         cat_q = keep.tile([P, TILES, P], U32, align_bytes=64)
@@ -154,7 +159,7 @@ def tile_dynamicmemorybank_pa_s_kernel(tc, x, memory, w1, b1, out):
         for i in range(TILES):
             cat_words = cat[:, i, :].bitcast(F32).rearrange("p (q u) -> p u q", u=PAIR)
             flipped = transpose_pair([cat_words[:, u, :] for u in range(PAIR)])
-            copy_out(i, cat_grp[:, i], flipped[:].rearrange("q u t -> q t u"))
+            nc.vector.tensor_copy(out=cat_grp[:, i], in_=flipped[:].rearrange("q u t -> q t u"))
             nc.vector.quantize_mx(
                 out=cat_q[:, i, :].bitcast(FP8X4),
                 scales=cat_s[:, i, :],
@@ -175,6 +180,9 @@ def tile_dynamicmemorybank_pa_s_kernel(tc, x, memory, w1, b1, out):
                 start=True,
                 stop=True,
             )
-            nc.vector.tensor_tensor(out=biased[:, i, :], in0=fused[:], in1=b1_all[:], op=ALU.add)
-            nc.scalar.activation(out=result[:, i, :], in_=biased[:, i, :], func=ACT.Silu)
-            nc.sync.dma_start(out=out_rows[:, i, :], in_=result[:, i, :])
+            for half in (slice(0, F // 2), slice(F // 2, F)):
+                nc.vector.tensor_tensor(
+                    out=biased[:, i, half], in0=fused[:, half], in1=b1_all[:, half], op=ALU.add
+                )
+                nc.scalar.activation(out=result[:, i, half], in_=biased[:, i, half], func=ACT.Silu)
+                nc.sync.dma_start(out=out_rows[:, i, half], in_=result[:, i, half])

@@ -17,6 +17,7 @@ PACK = 4
 T, C, M, F = 512, 256, 512, 512
 TILES = T // P
 PAIR = 2
+RUN = 4
 VECTOR_TILES = 2
 
 FLOPS = 2 * T * M * C + 2 * T * M * C + 2 * T * (2 * C) * F
@@ -81,7 +82,10 @@ def tile_dynamicmemorybank_pa_s_kernel(tc, x, memory, w1, b1, out):
         mem_grp = keep.tile([P, C, PACK], BF16, align_bytes=64)
         mem_q = keep.tile([P, C], U32, align_bytes=64)
         mem_s = keep.tile([P, C], U8, align_bytes=64)
-        nc.vector.tensor_copy(out=mem_grp[:], in_=mem_sb[:].rearrange("p j c -> p c j"))
+        nc.vector.tensor_copy(
+            out=mem_grp[:].rearrange("p (c r) j -> p c j r", r=RUN),
+            in_=mem_sb[:].rearrange("p j (c r) -> p c j r", r=RUN),
+        )
         nc.vector.quantize_mx(
             out=mem_q[:].bitcast(FP8X4), scales=mem_s[:], in_=mem_grp[:].rearrange("p c j -> p (c j)")
         )
@@ -89,7 +93,10 @@ def tile_dynamicmemorybank_pa_s_kernel(tc, x, memory, w1, b1, out):
         w1_grp = keep.tile([P, F, PACK], BF16, align_bytes=64)
         w1_q = keep.tile([P, F], U32, align_bytes=64)
         w1_s = keep.tile([P, F], U8, align_bytes=64)
-        nc.vector.tensor_copy(out=w1_grp[:], in_=w1_sb[:].rearrange("p j f -> p f j"))
+        nc.vector.tensor_copy(
+            out=w1_grp[:].rearrange("p (f r) j -> p f j r", r=RUN),
+            in_=w1_sb[:].rearrange("p j (f r) -> p f j r", r=RUN),
+        )
         nc.vector.quantize_mx(
             out=w1_q[:].bitcast(FP8X4), scales=w1_s[:], in_=w1_grp[:].rearrange("p f j -> p (f j)")
         )

@@ -18,7 +18,6 @@ T, C, M, F = 512, 256, 512, 512
 TILES = T // P
 PAIR = 2
 RUN = 4
-VECTOR_TILES = 2
 
 FLOPS = 2 * T * M * C + 2 * T * M * C + 2 * T * (2 * C) * F
 
@@ -29,25 +28,50 @@ def tile_dynamicmemorybank_pa_s_kernel(tc, x, memory, w1, b1, out):
         keep = ctx.enter_context(tc.tile_pool(name="keep", bufs=1))
         turned = ctx.enter_context(tc.psum_pool(name="turned", bufs=4))
         sums = ctx.enter_context(tc.psum_pool(name="sums", bufs=4))
+        V, S = nc.vector.tensor_copy, nc.scalar.copy
 
         mem_sb = keep.tile([P, PACK, C], BF16)
         mem_rows = memory[0].rearrange("(p j) c -> p j c", j=PACK)
         cat = keep.tile([P, TILES, 2 * C], BF16)
         x_rows = x[0].rearrange("(p i) c -> p i c", i=TILES)
-        nc.sync.dma_start(out=mem_sb[:, 0:PAIR, :], in_=mem_rows[:, 0:PAIR, :])
-        nc.sync.dma_start(out=mem_sb[:, PAIR:PACK, :], in_=mem_rows[:, PAIR:PACK, :])
-        nc.sync.dma_start(out=cat[:, 0:PAIR, 0:C], in_=x_rows[:, 0:PAIR, :])
-        nc.sync.dma_start(out=cat[:, PAIR:TILES, 0:C], in_=x_rows[:, PAIR:TILES, :])
         w1_sb = keep.tile([P, PACK, F], BF16)
-        nc.sync.dma_start(out=w1_sb[:], in_=w1.rearrange("(p j) f -> p j f", j=PACK))
         b1_all = keep.tile([P, F], BF16)
-        nc.sync.dma_start(out=b1_all[:], in_=b1.partition_broadcast(P))
-
         ident = keep.tile([P, P], F32)
-        make_identity(nc, ident[:])
-
         warm_in = keep.tile([P, 1], F32)
         warm_out = keep.tile([P, PAIR], F32)
+        memT = keep.tile([P, M], F32)
+        xT = keep.tile([P, T], F32)
+        mem_grp = keep.tile([P, C, PACK], BF16, align_bytes=64)
+        mem_q = keep.tile([P, C], U32, align_bytes=64)
+        mem_s = keep.tile([P, C], U8, align_bytes=64)
+        w1_grp = keep.tile([P, F, PACK], BF16, align_bytes=64)
+        w1_q = keep.tile([P, F], U32, align_bytes=64)
+        w1_s = keep.tile([P, F], U8, align_bytes=64)
+        neg_max = keep.tile([P, TILES], F32)
+        row_sum = keep.tile([P, TILES], F32)
+        inv_sum = keep.tile([P, TILES], F32)
+        e_sb = keep.tile([P, TILES, M], BF16)
+        e_grp = keep.tile([P, TILES, P, PAIR], F32, align_bytes=64)
+        e_q = keep.tile([P, TILES, P], U32, align_bytes=64)
+        e_s = keep.tile([P, TILES, P], U8, align_bytes=64)
+        cat_grp = keep.tile([P, TILES, P, PAIR], F32, align_bytes=64)
+        cat_q = keep.tile([P, TILES, P], U32, align_bytes=64)
+        cat_s = keep.tile([P, TILES, P], U8, align_bytes=64)
+        out_rows = out[0].rearrange("(p i) f -> p i f", i=TILES)
+        biased = keep.tile([P, TILES, F], F32)
+        result = keep.tile([P, TILES, F], F32)
+        memT_half = memT[:].bitcast(BF16).rearrange("w (m h) -> w h m", h=PAIR)
+        xT_half = xT[:].bitcast(BF16).rearrange("w (t h) -> w h t", h=PAIR)
+        energies, reads, fuseds, tx_ps, tm_ps, te_ps, tc_ps = {}, {}, {}, {}, {}, {}, {}
+
+        nc.sync.dma_start(out=cat[:, 0:1, 0:C], in_=x_rows[:, 0:1, :])
+        nc.sync.dma_start(out=mem_sb[:, 0:PAIR, :], in_=mem_rows[:, 0:PAIR, :])
+        nc.sync.dma_start(out=mem_sb[:, PAIR:PACK, :], in_=mem_rows[:, PAIR:PACK, :])
+        nc.sync.dma_start(out=cat[:, 1:2, 0:C], in_=x_rows[:, 1:2, :])
+        nc.sync.dma_start(out=cat[:, PAIR:TILES, 0:C], in_=x_rows[:, PAIR:TILES, :])
+        nc.sync.dma_start(out=w1_sb[:], in_=w1.rearrange("(p j) f -> p j f", j=PACK))
+        nc.sync.dma_start(out=b1_all[:], in_=b1.partition_broadcast(P))
+        make_identity(nc, ident[:])
         nc.vector.memset(warm_in[:], 0.0)
         nc.scalar.activation(out=warm_out[:, 0:1], in_=warm_in[:], func=ACT.Exp)
 
@@ -57,94 +81,107 @@ def tile_dynamicmemorybank_pa_s_kernel(tc, x, memory, w1, b1, out):
                 nc.tensor.transpose(flipped[:, u, :], blocks[u], ident[:])
             return flipped
 
-        def copy_out(i, dst, src):
-            if i < VECTOR_TILES:
-                nc.vector.tensor_copy(out=dst, in_=src)
-            else:
-                nc.scalar.copy(out=dst, in_=src)
+        def tm(u):
+            tm_ps[u] = transpose_pair([mem_sb[:, PAIR * u + v, :].bitcast(F32) for v in range(PAIR)])
 
-        memT = keep.tile([P, M], F32)
-        for u in range(PAIR):
-            flipped = transpose_pair([mem_sb[:, PAIR * u + v, :].bitcast(F32) for v in range(PAIR)])
-            nc.scalar.copy(
+        def cm(u):
+            (nc.scalar.copy, nc.scalar.copy)[u](
                 out=memT[:, u * PAIR * P : (u + 1) * PAIR * P].rearrange("w (p v) -> w p v", v=PAIR),
-                in_=flipped[:].rearrange("w v p -> w p v"),
+                in_=tm_ps[u][:].rearrange("w v p -> w p v"),
             )
-        xT = keep.tile([P, T], F32)
-        for g in range(TILES // PAIR):
-            flipped = transpose_pair([cat[:, PAIR * g + r, 0:C].bitcast(F32) for r in range(PAIR)])
-            nc.scalar.copy(
-                out=xT[:, g * PAIR * P : (g + 1) * PAIR * P], in_=flipped[:].rearrange("w r p -> w (r p)")
+
+        def tx(i):
+            tx_ps[i] = turned.tile([P, P], F32, name="flipped", tag="flipped")
+            nc.tensor.transpose(tx_ps[i][:], cat[:, i, 0:C].bitcast(F32), ident[:])
+
+        def cx(i):
+            (S, S, S, S)[i](out=xT[:, i * P : (i + 1) * P], in_=tx_ps[i][:])
+
+        def txp(g):
+            tx_ps[4 + g] = transpose_pair([cat[:, PAIR * g + r, 0:C].bitcast(F32) for r in range(PAIR)])
+
+        def cxp(g):
+            nc.scalar.copy(out=xT[:, g * PAIR * P : (g + 1) * PAIR * P], in_=tx_ps[4 + g][:].rearrange("w r p -> w (r p)"))
+
+        def gm():
+            nc.vector.tensor_copy(
+                out=mem_grp[:].rearrange("p (c r) j -> p c j r", r=RUN),
+                in_=mem_sb[:].rearrange("p j (c r) -> p c j r", r=RUN),
             )
-        memT_half = memT[:].bitcast(BF16).rearrange("w (m h) -> w h m", h=PAIR)
-        xT_half = xT[:].bitcast(BF16).rearrange("w (t h) -> w h t", h=PAIR)
 
-        mem_grp = keep.tile([P, C, PACK], BF16, align_bytes=64)
-        mem_q = keep.tile([P, C], U32, align_bytes=64)
-        mem_s = keep.tile([P, C], U8, align_bytes=64)
-        nc.vector.tensor_copy(
-            out=mem_grp[:].rearrange("p (c r) j -> p c j r", r=RUN),
-            in_=mem_sb[:].rearrange("p j (c r) -> p c j r", r=RUN),
-        )
-        nc.vector.quantize_mx(
-            out=mem_q[:].bitcast(FP8X4), scales=mem_s[:], in_=mem_grp[:].rearrange("p c j -> p (c j)")
-        )
+        def qm():
+            nc.vector.quantize_mx(
+                out=mem_q[:].bitcast(FP8X4), scales=mem_s[:], in_=mem_grp[:].rearrange("p c j -> p (c j)")
+            )
 
-        w1_grp = keep.tile([P, F, PACK], BF16, align_bytes=64)
-        w1_q = keep.tile([P, F], U32, align_bytes=64)
-        w1_s = keep.tile([P, F], U8, align_bytes=64)
-        nc.vector.tensor_copy(
-            out=w1_grp[:].rearrange("p (f r) j -> p f j r", r=RUN),
-            in_=w1_sb[:].rearrange("p j (f r) -> p f j r", r=RUN),
-        )
-        nc.vector.quantize_mx(
-            out=w1_q[:].bitcast(FP8X4), scales=w1_s[:], in_=w1_grp[:].rearrange("p f j -> p (f j)")
-        )
+        def gw():
+            nc.gpsimd.tensor_scalar(
+                out=w1_grp[:], in0=w1_sb[:].rearrange("p j f -> p f j"), scalar1=1.0, scalar2=0.0, op0=ALU.mult, op1=ALU.add
+            )
 
-        neg_max = keep.tile([P, TILES], F32)
-        row_sum = keep.tile([P, TILES], F32)
-        inv_sum = keep.tile([P, TILES], F32)
-        e_sb = keep.tile([P, TILES, M], BF16)
-        for i in range(TILES):
-            energy = sums.tile([P, M], F32, name="energy", tag="sums")
+        def qw():
+            nc.vector.quantize_mx(
+                out=w1_q[:].bitcast(FP8X4), scales=w1_s[:], in_=w1_grp[:].rearrange("p f j -> p (f j)")
+            )
+
+        def energy_of(i):
+            if i not in energies:
+                energies[i] = sums.tile([P, M], F32, name="energy", tag="sums")
+            return energies[i]
+
+        def score(i, slots):
+            energy = energy_of(i)
             for h in range(PAIR):
                 nc.tensor.matmul(
-                    energy[:],
+                    energy[:, slots],
                     lhsT=xT_half[:, h, i * P : (i + 1) * P],
-                    rhs=memT_half[:, h, :],
+                    rhs=memT_half[:, h, slots],
                     start=(h == 0),
                     stop=(h == PAIR - 1),
                 )
+
+        def sh(half):
+            score(0, slice(half * M // 2, (half + 1) * M // 2))
+
+        def sc(i):
+            score(i, slice(0, M))
+
+        def mx(i):
             nc.vector.tensor_reduce(
-                out=neg_max[:, i : i + 1], in_=energy[:], axis=AXIS.X, op=ALU.max, negate=True
+                out=neg_max[:, i : i + 1], in_=energies[i][:], axis=AXIS.X, op=ALU.max, negate=True
             )
+
+        def ex(i):
             nc.scalar.activation(
                 out=e_sb[:, i, :],
-                in_=energy[:],
+                in_=energies[i][:],
                 func=ACT.Exp,
                 bias=neg_max[:, i : i + 1],
                 scale=1.0,
                 accum_out=row_sum[:, i : i + 1],
             )
+
+        def rc(i):
             nc.vector.reciprocal(inv_sum[:, i : i + 1], row_sum[:, i : i + 1])
 
-        e_grp = keep.tile([P, TILES, P, PAIR], F32, align_bytes=64)
-        e_q = keep.tile([P, TILES, P], U32, align_bytes=64)
-        e_s = keep.tile([P, TILES, P], U8, align_bytes=64)
-        for i in range(TILES):
+        def te(i):
             e_words = e_sb[:, i, :].bitcast(F32)
-            flipped = transpose_pair([e_words[:, u * P : (u + 1) * P] for u in range(PAIR)])
-            copy_out(i, e_grp[:, i], flipped[:].rearrange("p u t -> p t u"))
+            te_ps[i] = transpose_pair([e_words[:, u * P : (u + 1) * P] for u in range(PAIR)])
+
+        def ce(i):
+            (V, V, V, V)[i](out=e_grp[:, i], in_=te_ps[i][:].rearrange("p u t -> p t u"))
+
+        def qe(i):
             nc.vector.quantize_mx(
                 out=e_q[:, i, :].bitcast(FP8X4),
                 scales=e_s[:, i, :],
                 in_=e_grp[:, i].rearrange("p t u -> p (t u)").bitcast(BF16),
             )
 
-        for i in range(TILES):
-            read = sums.tile([P, C], F32, name="read", tag="sums")
+        def m(i):
+            reads[i] = sums.tile([P, C], F32, name="read", tag="sums")
             nc.tensor.matmul_mx(
-                out=read[:],
+                out=reads[i][:],
                 lhsT=e_q[:, i, :].bitcast(FP8X4),
                 lhsT_scale=e_s[:, i, :],
                 rhs=mem_q[:].bitcast(FP8X4),
@@ -152,34 +189,36 @@ def tile_dynamicmemorybank_pa_s_kernel(tc, x, memory, w1, b1, out):
                 start=True,
                 stop=True,
             )
-            nc.scalar.activation(
-                out=cat[:, i, C : 2 * C],
-                in_=read[:],
-                func=ACT.Copy,
-                scale=inv_sum[:, i : i + 1],
-            )
-        nc.scalar.activation(out=warm_out[:, 1:2], in_=cat[:, TILES - 1, 2 * C - 1 : 2 * C], func=ACT.Silu)
 
-        cat_grp = keep.tile([P, TILES, P, PAIR], F32, align_bytes=64)
-        cat_q = keep.tile([P, TILES, P], U32, align_bytes=64)
-        cat_s = keep.tile([P, TILES, P], U8, align_bytes=64)
-        for i in range(TILES):
+        def nr(i):
+            if "VVSS"[i] == "S":
+                nc.scalar.activation(
+                    out=cat[:, i, C : 2 * C], in_=reads[i][:], func=ACT.Copy, scale=inv_sum[:, i : i + 1]
+                )
+            else:
+                nc.vector.tensor_scalar_mul(cat[:, i, C : 2 * C], reads[i][:], inv_sum[:, i : i + 1])
+
+        def tS():
+            nc.scalar.activation(out=warm_out[:, 1:2], in_=row_sum[:, TILES - 1 : TILES], func=ACT.Silu)
+
+        def tc2(i):
             cat_words = cat[:, i, :].bitcast(F32).rearrange("p (q u) -> p u q", u=PAIR)
-            flipped = transpose_pair([cat_words[:, u, :] for u in range(PAIR)])
-            nc.vector.tensor_copy(out=cat_grp[:, i], in_=flipped[:].rearrange("q u t -> q t u"))
+            tc_ps[i] = transpose_pair([cat_words[:, u, :] for u in range(PAIR)])
+
+        def cc(i):
+            (V, V, S, S)[i](out=cat_grp[:, i], in_=tc_ps[i][:].rearrange("q u t -> q t u"))
+
+        def qc(i):
             nc.vector.quantize_mx(
                 out=cat_q[:, i, :].bitcast(FP8X4),
                 scales=cat_s[:, i, :],
                 in_=cat_grp[:, i].rearrange("q t u -> q (t u)").bitcast(BF16),
             )
 
-        out_rows = out[0].rearrange("(p i) f -> p i f", i=TILES)
-        biased = keep.tile([P, TILES, F], F32)
-        result = keep.tile([P, TILES, F], F32)
-        for i in range(TILES):
-            fused = sums.tile([P, F], F32, name="fused", tag="sums")
+        def n(i):
+            fuseds[i] = sums.tile([P, F], F32, name="fused", tag="sums")
             nc.tensor.matmul_mx(
-                out=fused[:],
+                out=fuseds[i][:],
                 lhsT=cat_q[:, i, :].bitcast(FP8X4),
                 lhsT_scale=cat_s[:, i, :],
                 rhs=w1_q[:].bitcast(FP8X4),
@@ -187,9 +226,92 @@ def tile_dynamicmemorybank_pa_s_kernel(tc, x, memory, w1, b1, out):
                 start=True,
                 stop=True,
             )
+
+        def a(i):
             for half in (slice(0, F // 2), slice(F // 2, F)):
                 nc.vector.tensor_tensor(
-                    out=biased[:, i, half], in0=fused[:, half], in1=b1_all[:, half], op=ALU.add
+                    out=biased[:, i, half], in0=fuseds[i][:, half], in1=b1_all[:, half], op=ALU.add
                 )
+
+        def s(i):
+            for half in (slice(0, F // 2), slice(F // 2, F)):
                 nc.scalar.activation(out=result[:, i, half], in_=biased[:, i, half], func=ACT.Silu)
                 nc.sync.dma_start(out=out_rows[:, i, half], in_=result[:, i, half])
+
+        with tc.manual_schedule():
+            tx(0)
+            tm(0)
+            tm(1)
+            tx(1)
+            txp(1)
+            cx(0)
+            cm(0)
+            cm(1)
+            cx(1)
+            cxp(1)
+            gm()
+            qm()
+            gw()
+            sh(0)
+            sh(1)
+            sc(1)
+            sc(2)
+            sc(3)
+            mx(0)
+            ex(0)
+            mx(1)
+            ex(1)
+            mx(2)
+            ex(2)
+            mx(3)
+            ex(3)
+            te(0)
+            ce(0)
+            te(1)
+            te(2)
+            tS()
+            rc(0)
+            qe(0)
+            rc(1)
+            ce(1)
+            m(0)
+            rc(2)
+            ce(2)
+            qe(1)
+            te(3)
+            rc(3)
+            nr(0)
+            m(1)
+            tc2(0)
+            qe(2)
+            ce(3)
+            nr(1)
+            m(2)
+            tc2(1)
+            qe(3)
+            cc(0)
+            m(3)
+            qw()
+            nr(2)
+            cc(1)
+            qc(0)
+            nr(3)
+            tc2(2)
+            n(0)
+            tc2(3)
+            cc(2)
+            cc(3)
+            qc(1)
+            n(1)
+            qc(2)
+            n(2)
+            a(0)
+            qc(3)
+            n(3)
+            s(0)
+            a(1)
+            s(1)
+            a(2)
+            s(2)
+            a(3)
+            s(3)

@@ -75,6 +75,14 @@ def tile_dynamicmemorybank_pa_s_kernel(tc, x, memory, w1, b1, out):
         nc.vector.memset(warm_in[:], 0.0)
         nc.scalar.activation(out=warm_out[:, 0:1], in_=warm_in[:], func=ACT.Exp)
 
+        zeros = keep.tile([P, P], F32)
+        nc.vector.memset(zeros[:], 0.0)
+
+        def dummy(k):
+            for turn in range(k):
+                idle = turned.tile([P, P], F32, name="flipped", tag="flipped")
+                nc.tensor.matmul(idle[:], lhsT=zeros[:], rhs=zeros[:], start=True, stop=True)
+
         def transpose_pair(blocks):
             flipped = turned.tile([P, PAIR, P], F32, name="flipped", tag="flipped")
             for u in range(PAIR):
@@ -239,6 +247,7 @@ def tile_dynamicmemorybank_pa_s_kernel(tc, x, memory, w1, b1, out):
                 nc.sync.dma_start(out=out_rows[:, i, half], in_=result[:, i, half])
 
         with tc.manual_schedule():
+            dummy(3)
             tx(0)
             tm(0)
             tm(1)

@@ -71,17 +71,18 @@ def tile_dynamicmemorybank_pa_s_kernel(tc, x, memory, w1, b1, out):
         nc.sync.dma_start(out=cat[:, PAIR:TILES, 0:C], in_=x_rows[:, PAIR:TILES, :])
         nc.sync.dma_start(out=w1_sb[:], in_=w1.rearrange("(p j) f -> p j f", j=PACK))
         nc.sync.dma_start(out=b1_all[:], in_=b1.partition_broadcast(P))
+
+        zeros = keep.tile([P, P], F32)
+        nc.gpsimd.memset(zeros[:], 0.0)
+
         make_identity(nc, ident[:])
         nc.vector.memset(warm_in[:], 0.0)
         nc.scalar.activation(out=warm_out[:, 0:1], in_=warm_in[:], func=ACT.Exp)
 
-        zeros = keep.tile([P, P], F32)
-        nc.vector.memset(zeros[:], 0.0)
-
-        def dummy(k):
+        def dummy(k, width=P):
             for turn in range(k):
-                idle = turned.tile([P, P], F32, name="flipped", tag="flipped")
-                nc.tensor.matmul(idle[:], lhsT=zeros[:], rhs=zeros[:], start=True, stop=True)
+                idle = turned.tile([P, width], F32, name="flipped", tag="flipped")
+                nc.tensor.matmul(idle[:], lhsT=zeros[:], rhs=zeros[:, 0:width], start=True, stop=True)
 
         def transpose_pair(blocks):
             flipped = turned.tile([P, PAIR, P], F32, name="flipped", tag="flipped")
@@ -214,7 +215,7 @@ def tile_dynamicmemorybank_pa_s_kernel(tc, x, memory, w1, b1, out):
             tc_ps[i] = transpose_pair([cat_words[:, u, :] for u in range(PAIR)])
 
         def cc(i):
-            (V, V, S, S)[i](out=cat_grp[:, i], in_=tc_ps[i][:].rearrange("q u t -> q t u"))
+            (S, S, S, S)[i](out=cat_grp[:, i], in_=tc_ps[i][:].rearrange("q u t -> q t u"))
 
         def qc(i):
             nc.vector.quantize_mx(
@@ -247,7 +248,7 @@ def tile_dynamicmemorybank_pa_s_kernel(tc, x, memory, w1, b1, out):
                 nc.sync.dma_start(out=out_rows[:, i, half], in_=result[:, i, half])
 
         with tc.manual_schedule():
-            dummy(3)
+            dummy(4)
             tx(0)
             tm(0)
             tm(1)
@@ -270,55 +271,55 @@ def tile_dynamicmemorybank_pa_s_kernel(tc, x, memory, w1, b1, out):
             ex(0)
             mx(1)
             ex(1)
+            te(0)
             mx(2)
             ex(2)
+            te(1)
             mx(3)
             ex(3)
-            te(0)
             ce(0)
-            te(1)
-            te(2)
-            tS()
             rc(0)
-            qe(0)
             rc(1)
+            qe(0)
+            tS()
+            te(2)
             ce(1)
             m(0)
             rc(2)
-            ce(2)
             qe(1)
+            ce(2)
             te(3)
-            rc(3)
-            nr(0)
             m(1)
-            tc2(0)
+            nr(0)
             qe(2)
-            ce(3)
             nr(1)
             m(2)
-            tc2(1)
+            ce(3)
+            tc2(0)
+            rc(3)
             qe(3)
-            cc(0)
-            m(3)
-            qw()
+            tc2(1)
             nr(2)
+            m(3)
+            cc(0)
+            qw()
+            tc2(2)
             cc(1)
             qc(0)
             nr(3)
-            tc2(2)
             n(0)
-            tc2(3)
             cc(2)
-            cc(3)
             qc(1)
+            tc2(3)
             n(1)
             qc(2)
-            n(2)
+            cc(3)
             a(0)
+            n(2)
             qc(3)
-            n(3)
             s(0)
             a(1)
+            n(3)
             s(1)
             a(2)
             s(2)

@@ -26,7 +26,8 @@ def tile_dynamicmemorybank_pa_s_kernel(tc, x, memory, w1, b1, out):
     nc = tc.nc
     with ExitStack() as ctx:
         keep = ctx.enter_context(tc.tile_pool(name="keep", bufs=1))
-        turned = ctx.enter_context(tc.psum_pool(name="turned", bufs=4))
+        turned = ctx.enter_context(tc.psum_pool(name="turned", bufs=3))
+        unread = ctx.enter_context(tc.psum_pool(name="unread", bufs=1))
         sums = ctx.enter_context(tc.psum_pool(name="sums", bufs=4))
         V, S = nc.vector.tensor_copy, nc.scalar.copy
 
@@ -81,7 +82,7 @@ def tile_dynamicmemorybank_pa_s_kernel(tc, x, memory, w1, b1, out):
 
         def dummy(k, width=P):
             for turn in range(k):
-                idle = turned.tile([P, width], F32, name="flipped", tag="flipped")
+                idle = unread.tile([P, width], F32, name="idle", tag="idle")
                 nc.tensor.matmul(idle[:], lhsT=zeros[:], rhs=zeros[:, 0:width], start=True, stop=True)
 
         def transpose_pair(blocks):
@@ -100,7 +101,7 @@ def tile_dynamicmemorybank_pa_s_kernel(tc, x, memory, w1, b1, out):
             )
 
         def tx(i):
-            tx_ps[i] = turned.tile([P, P], F32, name="flipped", tag="flipped")
+            tx_ps[i] = sums.tile([P, P], F32, name="x_turned", tag="sums")
             nc.tensor.transpose(tx_ps[i][:], cat[:, i, 0:C].bitcast(F32), ident[:])
 
         def cx(i):
@@ -248,7 +249,7 @@ def tile_dynamicmemorybank_pa_s_kernel(tc, x, memory, w1, b1, out):
                 nc.sync.dma_start(out=out_rows[:, i, half], in_=result[:, i, half])
 
         with tc.manual_schedule():
-            dummy(4)
+            dummy(3)
             tx(0)
             tm(0)
             tm(1)
@@ -272,9 +273,11 @@ def tile_dynamicmemorybank_pa_s_kernel(tc, x, memory, w1, b1, out):
             mx(1)
             ex(1)
             te(0)
+            dummy(1, P // 2)
             mx(2)
             ex(2)
             te(1)
+            dummy(1, P // 2)
             mx(3)
             ex(3)
             ce(0)
@@ -283,12 +286,14 @@ def tile_dynamicmemorybank_pa_s_kernel(tc, x, memory, w1, b1, out):
             qe(0)
             tS()
             te(2)
+            dummy(1, P // 2)
             ce(1)
             m(0)
             rc(2)
             qe(1)
             ce(2)
             te(3)
+            dummy(1, P // 2)
             m(1)
             nr(0)
             qe(2)

@@ -82,7 +82,10 @@ def tile_dynamicmemorybank_pa_s_kernel(tc, x, memory, w1, b1, out):
 
         def dummy(k, width=P):
             for turn in range(k):
-                idle = unread.tile([P, width], F32, name="idle", tag="idle")
+                if width == P:
+                    idle = turned.tile([P, P], F32, name="flipped", tag="flipped")
+                else:
+                    idle = unread.tile([P, width], F32, name="idle", tag="idle")
                 nc.tensor.matmul(idle[:], lhsT=zeros[:], rhs=zeros[:, 0:width], start=True, stop=True)
 
         def transpose_pair(blocks):
@@ -250,6 +253,7 @@ def tile_dynamicmemorybank_pa_s_kernel(tc, x, memory, w1, b1, out):
 
         with tc.manual_schedule():
             dummy(3)
+            dummy(1, P // 2)
             tx(0)
             tm(0)
             tm(1)
@@ -293,7 +297,6 @@ def tile_dynamicmemorybank_pa_s_kernel(tc, x, memory, w1, b1, out):
             qe(1)
             ce(2)
             te(3)
-            dummy(1, P // 2)
             m(1)
             nr(0)
             qe(2)

@@ -94,14 +94,13 @@ def tile_dynamicmemorybank_pa_s_kernel(tc, x, memory, w1, b1, out):
                 nc.tensor.transpose(flipped[:, u, :], blocks[u], ident[:])
             return flipped
 
-        def tm(u):
-            tm_ps[u] = transpose_pair([mem_sb[:, PAIR * u + v, :].bitcast(F32) for v in range(PAIR)])
+        def tb(j):
+            pool, tag = (sums, "sums") if j == PACK - 1 else (turned, "flipped")
+            tm_ps[j] = pool.tile([P, P], F32, name="mem_turned", tag=tag)
+            nc.tensor.transpose(tm_ps[j][:], mem_sb[:, j, :].bitcast(F32), ident[:])
 
-        def cm(u):
-            (nc.scalar.copy, nc.scalar.copy)[u](
-                out=memT[:, u * PAIR * P : (u + 1) * PAIR * P].rearrange("w (p v) -> w p v", v=PAIR),
-                in_=tm_ps[u][:].rearrange("w v p -> w p v"),
-            )
+        def cb(j):
+            S(out=memT[:, j * P : (j + 1) * P], in_=tm_ps[j][:])
 
         def tx(i):
             tx_ps[i] = sums.tile([P, P], F32, name="x_turned", tag="sums")
@@ -153,8 +152,8 @@ def tile_dynamicmemorybank_pa_s_kernel(tc, x, memory, w1, b1, out):
                     stop=(h == PAIR - 1),
                 )
 
-        def sh(half):
-            score(0, slice(half * M // 2, (half + 1) * M // 2))
+        def sg(j):
+            score(0, slice(0, PAIR * P) if j == 0 else slice(j * P, (j + 1) * P))
 
         def sc(i):
             score(i, slice(0, M))
@@ -166,8 +165,8 @@ def tile_dynamicmemorybank_pa_s_kernel(tc, x, memory, w1, b1, out):
 
         def ex(i):
             nc.scalar.activation(
-                out=e_sb[:, i, :],
-                in_=energies[i][:],
+                out=e_sb[:, i, :].rearrange("t (u p v) -> t u p v", u=PAIR, v=PAIR),
+                in_=energies[i][:].rearrange("t (u v p) -> t u p v", u=PAIR, v=PAIR),
                 func=ACT.Exp,
                 bias=neg_max[:, i : i + 1],
                 scale=1.0,
@@ -177,12 +176,15 @@ def tile_dynamicmemorybank_pa_s_kernel(tc, x, memory, w1, b1, out):
         def rc(i):
             nc.vector.reciprocal(inv_sum[:, i : i + 1], row_sum[:, i : i + 1])
 
+        def rcp(g):
+            nc.vector.reciprocal(inv_sum[:, PAIR * g : PAIR * (g + 1)], row_sum[:, PAIR * g : PAIR * (g + 1)])
+
         def te(i):
             e_words = e_sb[:, i, :].bitcast(F32)
             te_ps[i] = transpose_pair([e_words[:, u * P : (u + 1) * P] for u in range(PAIR)])
 
         def ce(i):
-            (V, V, V, V)[i](out=e_grp[:, i], in_=te_ps[i][:].rearrange("p u t -> p t u"))
+            (V, V, S, S)[i](out=e_grp[:, i], in_=te_ps[i][:].rearrange("p u t -> p t u"))
 
         def qe(i):
             nc.vector.quantize_mx(
@@ -204,7 +206,7 @@ def tile_dynamicmemorybank_pa_s_kernel(tc, x, memory, w1, b1, out):
             )
 
         def nr(i):
-            if "VVSS"[i] == "S":
+            if "VSVV"[i] == "S":
                 nc.scalar.activation(
                     out=cat[:, i, C : 2 * C], in_=reads[i][:], func=ACT.Copy, scale=inv_sum[:, i : i + 1]
                 )
@@ -219,7 +221,7 @@ def tile_dynamicmemorybank_pa_s_kernel(tc, x, memory, w1, b1, out):
             tc_ps[i] = transpose_pair([cat_words[:, u, :] for u in range(PAIR)])
 
         def cc(i):
-            (S, S, S, S)[i](out=cat_grp[:, i], in_=tc_ps[i][:].rearrange("q u t -> q t u"))
+            (S, V, V, S)[i](out=cat_grp[:, i], in_=tc_ps[i][:].rearrange("q u t -> q t u"))
 
         def qc(i):
             nc.vector.quantize_mx(
@@ -255,20 +257,25 @@ def tile_dynamicmemorybank_pa_s_kernel(tc, x, memory, w1, b1, out):
             dummy(3)
             dummy(1, P // 2)
             tx(0)
-            tm(0)
-            tm(1)
+            tb(0)
+            tb(1)
+            tb(2)
+            tb(3)
             tx(1)
             txp(1)
             cx(0)
-            cm(0)
-            cm(1)
+            cb(0)
+            cb(1)
+            cb(2)
+            cb(3)
             cx(1)
             cxp(1)
             gm()
             qm()
             gw()
-            sh(0)
-            sh(1)
+            sg(0)
+            sg(2)
+            sg(3)
             sc(1)
             sc(2)
             sc(3)
@@ -285,50 +292,50 @@ def tile_dynamicmemorybank_pa_s_kernel(tc, x, memory, w1, b1, out):
             mx(3)
             ex(3)
             ce(0)
-            rc(0)
-            rc(1)
             qe(0)
-            tS()
             te(2)
             dummy(1, P // 2)
             ce(1)
+            rcp(0)
             m(0)
-            rc(2)
+            te(3)
             qe(1)
             ce(2)
-            te(3)
-            m(1)
             nr(0)
-            qe(2)
-            nr(1)
-            m(2)
+            rcp(1)
             ce(3)
+            m(1)
+            dummy(1, P // 2)
+            qe(2)
             tc2(0)
-            rc(3)
-            qe(3)
-            tc2(1)
-            nr(2)
-            m(3)
-            cc(0)
             qw()
+            m(2)
+            qe(3)
+            nr(2)
+            nr(1)
+            tc2(1)
+            m(3)
+            dummy(1, P // 2)
+            cc(0)
             tc2(2)
-            cc(1)
             qc(0)
-            nr(3)
             n(0)
-            cc(2)
-            qc(1)
+            cc(1)
+            tS()
+            nr(3)
             tc2(3)
+            cc(2)
+            cc(3)
+            qc(1)
             n(1)
             qc(2)
-            cc(3)
-            a(0)
             n(2)
+            a(0)
             qc(3)
             s(0)
             a(1)
-            n(3)
             s(1)
+            n(3)
             a(2)
             s(2)
             a(3)

@@ -70,7 +70,9 @@ def tile_dynamicmemorybank_pa_s_kernel(tc, x, memory, w1, b1, out):
         nc.sync.dma_start(out=mem_sb[:, PAIR:PACK, :], in_=mem_rows[:, PAIR:PACK, :])
         nc.sync.dma_start(out=cat[:, 1:2, 0:C], in_=x_rows[:, 1:2, :])
         nc.sync.dma_start(out=cat[:, PAIR:TILES, 0:C], in_=x_rows[:, PAIR:TILES, :])
-        nc.sync.dma_start(out=w1_sb[:], in_=w1.rearrange("(p j) f -> p j f", j=PACK))
+        w1_rows = w1.rearrange("(p j) f -> p j f", j=PACK)
+        for cols in (slice(0, F // 2), slice(F // 2, F)):
+            nc.sync.dma_start(out=w1_sb[:, :, cols], in_=w1_rows[:, :, cols])
         nc.sync.dma_start(out=b1_all[:], in_=b1.partition_broadcast(P))
 
         zeros = keep.tile([P, P], F32)
@@ -127,9 +129,15 @@ def tile_dynamicmemorybank_pa_s_kernel(tc, x, memory, w1, b1, out):
             )
 
         def gw():
-            nc.gpsimd.tensor_scalar(
-                out=w1_grp[:], in0=w1_sb[:].rearrange("p j f -> p f j"), scalar1=1.0, scalar2=0.0, op0=ALU.mult, op1=ALU.add
-            )
+            for cols in (slice(0, F // 2), slice(F // 2, F)):
+                nc.gpsimd.tensor_scalar(
+                    out=w1_grp[:, cols],
+                    in0=w1_sb[:, :, cols].rearrange("p j f -> p f j"),
+                    scalar1=1.0,
+                    scalar2=0.0,
+                    op0=ALU.mult,
+                    op1=ALU.add,
+                )
 
         def qw():
             nc.vector.quantize_mx(

@@ -38,7 +38,6 @@ def tile_dynamicmemorybank_pa_s_kernel(tc, x, memory, w1, b1, out):
         w1_sb = keep.tile([P, PACK, F], BF16)
         b1_all = keep.tile([P, F], BF16)
         ident = keep.tile([P, P], F32)
-        warm_in = keep.tile([P, 1], F32)
         warm_out = keep.tile([P, PAIR], F32)
         memT = keep.tile([P, M], F32)
         xT = keep.tile([P, T], F32)
@@ -75,12 +74,11 @@ def tile_dynamicmemorybank_pa_s_kernel(tc, x, memory, w1, b1, out):
             nc.sync.dma_start(out=w1_sb[:, :, cols], in_=w1_rows[:, :, cols])
         nc.sync.dma_start(out=b1_all[:], in_=b1.partition_broadcast(P))
 
-        zeros = keep.tile([P, P], F32)
+        zeros = keep.tile([P, 1], F32)
         nc.gpsimd.memset(zeros[:], 0.0)
 
         make_identity(nc, ident[:])
-        nc.vector.memset(warm_in[:], 0.0)
-        nc.scalar.activation(out=warm_out[:, 0:1], in_=warm_in[:], func=ACT.Exp)
+        nc.scalar.activation(out=warm_out[:, 0:1], in_=zeros[:], func=ACT.Exp)
 
         def dummy(k, width=P):
             for turn in range(k):
@@ -88,7 +86,13 @@ def tile_dynamicmemorybank_pa_s_kernel(tc, x, memory, w1, b1, out):
                     idle = turned.tile([P, P], F32, name="flipped", tag="flipped")
                 else:
                     idle = unread.tile([P, width], F32, name="idle", tag="idle")
-                nc.tensor.matmul(idle[:], lhsT=zeros[:], rhs=zeros[:, 0:width], start=True, stop=True)
+                nc.tensor.matmul(
+                    idle[:],
+                    lhsT=zeros[:].to_broadcast([P, P]),
+                    rhs=zeros[:].to_broadcast([P, width]),
+                    start=True,
+                    stop=True,
+                )
 
         def transpose_pair(blocks):
             flipped = turned.tile([P, PAIR, P], F32, name="flipped", tag="flipped")
@@ -269,6 +273,7 @@ def tile_dynamicmemorybank_pa_s_kernel(tc, x, memory, w1, b1, out):
             tb(1)
             tb(2)
             tb(3)
+            dummy(1, P // 2)
             tx(1)
             txp(1)
             cx(0)
@@ -302,10 +307,10 @@ def tile_dynamicmemorybank_pa_s_kernel(tc, x, memory, w1, b1, out):
             ce(0)
             qe(0)
             te(2)
-            dummy(1, P // 2)
             ce(1)
             rcp(0)
             m(0)
+            dummy(1, P // 2)
             te(3)
             qe(1)
             ce(2)
@@ -313,7 +318,6 @@ def tile_dynamicmemorybank_pa_s_kernel(tc, x, memory, w1, b1, out):
             rcp(1)
             ce(3)
             m(1)
-            dummy(1, P // 2)
             qe(2)
             tc2(0)
             qw()

@@ -33,7 +33,8 @@ def tile_dynamicmemorybank_pa_s_kernel(tc, x, memory, w1, b1, out):
 
         mem_sb = keep.tile([P, PACK, C], BF16)
         mem_rows = memory[0].rearrange("(p j) c -> p j c", j=PACK)
-        cat = keep.tile([P, TILES, 2 * C], BF16)
+        x_sb = keep.tile([P, TILES, C], BF16)
+        cat = keep.tile([P, TILES, PAIR, 2, C // PAIR // PAIR], F32)
         x_rows = x[0].rearrange("(p i) c -> p i c", i=TILES)
         w1_sb = keep.tile([P, PACK, F], BF16)
         b1_all = keep.tile([P, F], BF16)
@@ -64,11 +65,11 @@ def tile_dynamicmemorybank_pa_s_kernel(tc, x, memory, w1, b1, out):
         xT_half = xT[:].bitcast(BF16).rearrange("w (t h) -> w h t", h=PAIR)
         energies, reads, fuseds, tx_ps, tm_ps, te_ps, tc_ps = {}, {}, {}, {}, {}, {}, {}
 
-        nc.sync.dma_start(out=cat[:, 0:1, 0:C], in_=x_rows[:, 0:1, :])
+        nc.sync.dma_start(out=x_sb[:, 0:1, :], in_=x_rows[:, 0:1, :])
         nc.sync.dma_start(out=mem_sb[:, 0:PAIR, :], in_=mem_rows[:, 0:PAIR, :])
         nc.sync.dma_start(out=mem_sb[:, PAIR:PACK, :], in_=mem_rows[:, PAIR:PACK, :])
-        nc.sync.dma_start(out=cat[:, 1:2, 0:C], in_=x_rows[:, 1:2, :])
-        nc.sync.dma_start(out=cat[:, PAIR:TILES, 0:C], in_=x_rows[:, PAIR:TILES, :])
+        nc.sync.dma_start(out=x_sb[:, 1:2, :], in_=x_rows[:, 1:2, :])
+        nc.sync.dma_start(out=x_sb[:, PAIR:TILES, :], in_=x_rows[:, PAIR:TILES, :])
         w1_rows = w1.rearrange("(p j) f -> p j f", j=PACK)
         for cols in (slice(0, F // 2), slice(F // 2, F)):
             nc.sync.dma_start(out=w1_sb[:, :, cols], in_=w1_rows[:, :, cols])
@@ -110,13 +111,13 @@ def tile_dynamicmemorybank_pa_s_kernel(tc, x, memory, w1, b1, out):
 
         def tx(i):
             tx_ps[i] = sums.tile([P, P], F32, name="x_turned", tag="sums")
-            nc.tensor.transpose(tx_ps[i][:], cat[:, i, 0:C].bitcast(F32), ident[:])
+            nc.tensor.transpose(tx_ps[i][:], x_sb[:, i, :].bitcast(F32), ident[:])
 
         def cx(i):
             (S, S, S, S)[i](out=xT[:, i * P : (i + 1) * P], in_=tx_ps[i][:])
 
         def txp(g):
-            tx_ps[4 + g] = transpose_pair([cat[:, PAIR * g + r, 0:C].bitcast(F32) for r in range(PAIR)])
+            tx_ps[4 + g] = transpose_pair([x_sb[:, PAIR * g + r, :].bitcast(F32) for r in range(PAIR)])
 
         def cxp(g):
             nc.scalar.copy(out=xT[:, g * PAIR * P : (g + 1) * PAIR * P], in_=tx_ps[4 + g][:].rearrange("w r p -> w (r p)"))
@@ -218,19 +219,24 @@ def tile_dynamicmemorybank_pa_s_kernel(tc, x, memory, w1, b1, out):
             )
 
         def nr(i):
+            target = cat[:, i, :, 1, :].bitcast(BF16).rearrange("p u (q e) -> p u q e", e=PAIR)
+            source = reads[i][:].rearrange("p (q u e) -> p u q e", u=PAIR, e=PAIR)
             if "VSVV"[i] == "S":
-                nc.scalar.activation(
-                    out=cat[:, i, C : 2 * C], in_=reads[i][:], func=ACT.Copy, scale=inv_sum[:, i : i + 1]
-                )
+                nc.scalar.activation(out=target, in_=source, func=ACT.Copy, scale=inv_sum[:, i : i + 1])
             else:
-                nc.vector.tensor_scalar_mul(cat[:, i, C : 2 * C], reads[i][:], inv_sum[:, i : i + 1])
+                nc.vector.tensor_scalar_mul(target, source, inv_sum[:, i : i + 1])
+
+        def xp():
+            nc.scalar.copy(
+                out=cat[:, :, :, 0, :],
+                in_=x_sb[:].rearrange("p i c -> p (i c)").bitcast(F32).rearrange("p (i q u) -> p i u q", i=TILES, u=PAIR),
+            )
 
         def tS():
             nc.scalar.activation(out=warm_out[:, 1:2], in_=row_sum[:, TILES - 1 : TILES], func=ACT.Silu)
 
         def tc2(i):
-            cat_words = cat[:, i, :].bitcast(F32).rearrange("p (q u) -> p u q", u=PAIR)
-            tc_ps[i] = transpose_pair([cat_words[:, u, :] for u in range(PAIR)])
+            tc_ps[i] = transpose_pair([cat[:, i, u].rearrange("p h q -> p (h q)") for u in range(PAIR)])
 
         def cc(i):
             (S, V, V, S)[i](out=cat_grp[:, i], in_=tc_ps[i][:].rearrange("q u t -> q t u"))
@@ -283,6 +289,7 @@ def tile_dynamicmemorybank_pa_s_kernel(tc, x, memory, w1, b1, out):
             cb(3)
             cx(1)
             cxp(1)
+            xp()
             gm()
             qm()
             gw()

from contextlib import ExitStack

import concourse.mybir as mybir
from concourse.masks import make_identity

BF16 = mybir.dt.bfloat16
F32 = mybir.dt.float32
U32 = mybir.dt.uint32
U8 = mybir.dt.uint8
FP8X4 = mybir.dt.float8_e4m3fn_x4
ACT = mybir.ActivationFunctionType
ALU = mybir.AluOpType
AXIS = mybir.AxisListType

P = 128
PACK = 4
T, C, M, F = 512, 256, 512, 512
TILES = T // P
PAIR = 2
RUN = 4

FLOPS = 2 * T * M * C + 2 * T * M * C + 2 * T * (2 * C) * F


def tile_dynamicmemorybank_pa_s_kernel(tc, x, memory, w1, b1, out):
    nc = tc.nc
    with ExitStack() as ctx:
        keep = ctx.enter_context(tc.tile_pool(name="keep", bufs=1))
        turned = ctx.enter_context(tc.psum_pool(name="turned", bufs=3))
        unread = ctx.enter_context(tc.psum_pool(name="unread", bufs=1))
        sums = ctx.enter_context(tc.psum_pool(name="sums", bufs=4))
        V, S = nc.vector.tensor_copy, nc.scalar.copy

        mem_sb = keep.tile([P, PACK, C], BF16)
        mem_rows = memory[0].rearrange("(p j) c -> p j c", j=PACK)
        x_sb = keep.tile([P, TILES, C], BF16)
        cat = keep.tile([P, TILES, PAIR, 2, C // PAIR // PAIR], F32)
        x_rows = x[0].rearrange("(p i) c -> p i c", i=TILES)
        w1_sb = keep.tile([P, PACK, F], BF16)
        b1_all = keep.tile([P, F], BF16)
        ident = keep.tile([P, P], F32)
        warm_out = keep.tile([P, PAIR], F32)
        memT = keep.tile([P, M], F32)
        xT = keep.tile([P, T], F32)
        mem_grp = keep.tile([P, C, PACK], BF16, align_bytes=64)
        mem_q = keep.tile([P, C], U32, align_bytes=64)
        mem_s = keep.tile([P, C], U8, align_bytes=64)
        w1_grp = keep.tile([P, F, PACK], BF16, align_bytes=64)
        w1_q = keep.tile([P, F], U32, align_bytes=64)
        w1_s = keep.tile([P, F], U8, align_bytes=64)
        neg_max = keep.tile([P, TILES], F32)
        row_sum = keep.tile([P, TILES], F32)
        inv_sum = keep.tile([P, TILES], F32)
        e_sb = keep.tile([P, TILES, M], BF16)
        e_grp = keep.tile([P, TILES, P, PAIR], F32, align_bytes=64)
        e_q = keep.tile([P, TILES, P], U32, align_bytes=64)
        e_s = keep.tile([P, TILES, P], U8, align_bytes=64)
        cat_grp = keep.tile([P, TILES, P, PAIR], F32, align_bytes=64)
        cat_q = keep.tile([P, TILES, P], U32, align_bytes=64)
        cat_s = keep.tile([P, TILES, P], U8, align_bytes=64)
        out_rows = out[0].rearrange("(p i) f -> p i f", i=TILES)
        biased = keep.tile([P, TILES, F], F32)
        result = keep.tile([P, TILES, F], F32)
        memT_half = memT[:].bitcast(BF16).rearrange("w (m h) -> w h m", h=PAIR)
        xT_half = xT[:].bitcast(BF16).rearrange("w (t h) -> w h t", h=PAIR)
        energies, reads, fuseds, tx_ps, tm_ps, te_ps, tc_ps = {}, {}, {}, {}, {}, {}, {}

        nc.sync.dma_start(out=x_sb[:, 0:1, :], in_=x_rows[:, 0:1, :])
        nc.sync.dma_start(out=mem_sb[:, 0:PAIR, :], in_=mem_rows[:, 0:PAIR, :])
        nc.sync.dma_start(out=mem_sb[:, PAIR:PACK, :], in_=mem_rows[:, PAIR:PACK, :])
        nc.sync.dma_start(out=x_sb[:, 1:2, :], in_=x_rows[:, 1:2, :])
        nc.sync.dma_start(out=x_sb[:, PAIR:TILES, :], in_=x_rows[:, PAIR:TILES, :])
        w1_rows = w1.rearrange("(p j) f -> p j f", j=PACK)
        for cols in (slice(0, F // 2), slice(F // 2, F)):
            nc.sync.dma_start(out=w1_sb[:, :, cols], in_=w1_rows[:, :, cols])
        nc.sync.dma_start(out=b1_all[:], in_=b1.partition_broadcast(P))

        zeros = keep.tile([P, 1], F32)
        nc.gpsimd.memset(zeros[:], 0.0)

        make_identity(nc, ident[:])
        nc.scalar.activation(out=warm_out[:, 0:1], in_=zeros[:], func=ACT.Exp)

        def dummy(k, width=P):
            for turn in range(k):
                if width == P:
                    idle = turned.tile([P, P], F32, name="flipped", tag="flipped")
                else:
                    idle = unread.tile([P, width], F32, name="idle", tag="idle")
                nc.tensor.matmul(
                    idle[:],
                    lhsT=zeros[:].to_broadcast([P, P]),
                    rhs=zeros[:].to_broadcast([P, width]),
                    start=True,
                    stop=True,
                )

        def transpose_pair(blocks):
            flipped = turned.tile([P, PAIR, P], F32, name="flipped", tag="flipped")
            for u in range(PAIR):
                nc.tensor.transpose(flipped[:, u, :], blocks[u], ident[:])
            return flipped

        def tb(j):
            pool, tag = (sums, "sums") if j == PACK - 1 else (turned, "flipped")
            tm_ps[j] = pool.tile([P, P], F32, name="mem_turned", tag=tag)
            nc.tensor.transpose(tm_ps[j][:], mem_sb[:, j, :].bitcast(F32), ident[:])

        def cb(j):
            S(out=memT[:, j * P : (j + 1) * P], in_=tm_ps[j][:])

        def tx(i):
            tx_ps[i] = sums.tile([P, P], F32, name="x_turned", tag="sums")
            nc.tensor.transpose(tx_ps[i][:], x_sb[:, i, :].bitcast(F32), ident[:])

        def cx(i):
            (S, S, S, S)[i](out=xT[:, i * P : (i + 1) * P], in_=tx_ps[i][:])

        def txp(g):
            tx_ps[4 + g] = transpose_pair([x_sb[:, PAIR * g + r, :].bitcast(F32) for r in range(PAIR)])

        def cxp(g):
            nc.scalar.copy(out=xT[:, g * PAIR * P : (g + 1) * PAIR * P], in_=tx_ps[4 + g][:].rearrange("w r p -> w (r p)"))

        def gm():
            nc.vector.tensor_copy(
                out=mem_grp[:].rearrange("p (c r) j -> p c j r", r=RUN),
                in_=mem_sb[:].rearrange("p j (c r) -> p c j r", r=RUN),
            )

        def qm():
            nc.vector.quantize_mx(
                out=mem_q[:].bitcast(FP8X4), scales=mem_s[:], in_=mem_grp[:].rearrange("p c j -> p (c j)")
            )

        def gw():
            for cols in (slice(0, F // 2), slice(F // 2, F)):
                nc.gpsimd.tensor_scalar(
                    out=w1_grp[:, cols],
                    in0=w1_sb[:, :, cols].rearrange("p j f -> p f j"),
                    scalar1=1.0,
                    scalar2=0.0,
                    op0=ALU.mult,
                    op1=ALU.add,
                )

        def qw():
            nc.vector.quantize_mx(
                out=w1_q[:].bitcast(FP8X4), scales=w1_s[:], in_=w1_grp[:].rearrange("p f j -> p (f j)")
            )

        def energy_of(i):
            if i not in energies:
                energies[i] = sums.tile([P, M], F32, name="energy", tag="sums")
            return energies[i]

        def score(i, slots):
            energy = energy_of(i)
            for h in range(PAIR):
                nc.tensor.matmul(
                    energy[:, slots],
                    lhsT=xT_half[:, h, i * P : (i + 1) * P],
                    rhs=memT_half[:, h, slots],
                    start=(h == 0),
                    stop=(h == PAIR - 1),
                )

        def sg(j):
            score(0, slice(0, PAIR * P) if j == 0 else slice(j * P, (j + 1) * P))

        def sc(i):
            score(i, slice(0, M))

        def mx(i):
            nc.vector.tensor_reduce(
                out=neg_max[:, i : i + 1], in_=energies[i][:], axis=AXIS.X, op=ALU.max, negate=True
            )

        def ex(i):
            nc.scalar.activation(
                out=e_sb[:, i, :].rearrange("t (u p v) -> t u p v", u=PAIR, v=PAIR),
                in_=energies[i][:].rearrange("t (u v p) -> t u p v", u=PAIR, v=PAIR),
                func=ACT.Exp,
                bias=neg_max[:, i : i + 1],
                scale=1.0,
                accum_out=row_sum[:, i : i + 1],
            )

        def rc(i):
            nc.vector.reciprocal(inv_sum[:, i : i + 1], row_sum[:, i : i + 1])

        def rcp(g):
            nc.vector.reciprocal(inv_sum[:, PAIR * g : PAIR * (g + 1)], row_sum[:, PAIR * g : PAIR * (g + 1)])

        def te(i):
            e_words = e_sb[:, i, :].bitcast(F32)
            te_ps[i] = transpose_pair([e_words[:, u * P : (u + 1) * P] for u in range(PAIR)])

        def ce(i):
            (V, V, S, S)[i](out=e_grp[:, i], in_=te_ps[i][:].rearrange("p u t -> p t u"))

        def qe(i):
            nc.vector.quantize_mx(
                out=e_q[:, i, :].bitcast(FP8X4),
                scales=e_s[:, i, :],
                in_=e_grp[:, i].rearrange("p t u -> p (t u)").bitcast(BF16),
            )

        def m(i):
            reads[i] = sums.tile([P, C], F32, name="read", tag="sums")
            nc.tensor.matmul_mx(
                out=reads[i][:],
                lhsT=e_q[:, i, :].bitcast(FP8X4),
                lhsT_scale=e_s[:, i, :],
                rhs=mem_q[:].bitcast(FP8X4),
                rhs_scale=mem_s[:],
                start=True,
                stop=True,
            )

        def nr(i):
            target = cat[:, i, :, 1, :].bitcast(BF16).rearrange("p u (q e) -> p u q e", e=PAIR)
            source = reads[i][:].rearrange("p (q u e) -> p u q e", u=PAIR, e=PAIR)
            if "VSVV"[i] == "S":
                nc.scalar.activation(out=target, in_=source, func=ACT.Copy, scale=inv_sum[:, i : i + 1])
            else:
                nc.vector.tensor_scalar_mul(target, source, inv_sum[:, i : i + 1])

        def xp():
            nc.scalar.copy(
                out=cat[:, :, :, 0, :],
                in_=x_sb[:].rearrange("p i c -> p (i c)").bitcast(F32).rearrange("p (i q u) -> p i u q", i=TILES, u=PAIR),
            )

        def tS():
            nc.scalar.activation(out=warm_out[:, 1:2], in_=row_sum[:, TILES - 1 : TILES], func=ACT.Silu)

        def tc2(i):
            tc_ps[i] = transpose_pair([cat[:, i, u].rearrange("p h q -> p (h q)") for u in range(PAIR)])

        def cc(i):
            (S, V, V, S)[i](out=cat_grp[:, i], in_=tc_ps[i][:].rearrange("q u t -> q t u"))

        def qc(i):
            nc.vector.quantize_mx(
                out=cat_q[:, i, :].bitcast(FP8X4),
                scales=cat_s[:, i, :],
                in_=cat_grp[:, i].rearrange("q t u -> q (t u)").bitcast(BF16),
            )

        def n(i):
            fuseds[i] = sums.tile([P, F], F32, name="fused", tag="sums")
            nc.tensor.matmul_mx(
                out=fuseds[i][:],
                lhsT=cat_q[:, i, :].bitcast(FP8X4),
                lhsT_scale=cat_s[:, i, :],
                rhs=w1_q[:].bitcast(FP8X4),
                rhs_scale=w1_s[:],
                start=True,
                stop=True,
            )

        def a(i):
            for half in (slice(0, F // 2), slice(F // 2, F)):
                nc.vector.tensor_tensor(
                    out=biased[:, i, half], in0=fuseds[i][:, half], in1=b1_all[:, half], op=ALU.add
                )

        def s(i):
            for half in (slice(0, F // 2), slice(F // 2, F)):
                nc.scalar.activation(out=result[:, i, half], in_=biased[:, i, half], func=ACT.Silu)
                nc.sync.dma_start(out=out_rows[:, i, half], in_=result[:, i, half])

        with tc.manual_schedule():
            dummy(3)
            dummy(1, P // 2)
            tx(0)
            tb(0)
            tb(1)
            tb(2)
            tb(3)
            dummy(1, P // 2)
            tx(1)
            txp(1)
            cx(0)
            cb(0)
            cb(1)
            cb(2)
            cb(3)
            cx(1)
            cxp(1)
            xp()
            gm()
            qm()
            gw()
            sg(0)
            sg(2)
            sg(3)
            sc(1)
            sc(2)
            sc(3)
            mx(0)
            ex(0)
            mx(1)
            ex(1)
            te(0)
            dummy(1, P // 2)
            mx(2)
            ex(2)
            te(1)
            dummy(1, P // 2)
            mx(3)
            ex(3)
            ce(0)
            qe(0)
            te(2)
            ce(1)
            rcp(0)
            m(0)
            dummy(1, P // 2)
            te(3)
            qe(1)
            ce(2)
            nr(0)
            rcp(1)
            ce(3)
            m(1)
            qe(2)
            tc2(0)
            qw()
            m(2)
            qe(3)
            nr(2)
            nr(1)
            tc2(1)
            m(3)
            dummy(1, P // 2)
            cc(0)
            tc2(2)
            qc(0)
            n(0)
            cc(1)
            tS()
            nr(3)
            tc2(3)
            cc(2)
            cc(3)
            qc(1)
            n(1)
            qc(2)
            n(2)
            a(0)
            qc(3)
            s(0)
            a(1)
            s(1)
            n(3)
            a(2)
            s(2)
            a(3)
            s(3)
